import numpy as np
import ml_dtypes


def mxq(x, axis, fmt="e4m3"):
    dtype, down = {"e4m3": (ml_dtypes.float8_e4m3fn, 7), "e5m2": (ml_dtypes.float8_e5m2, 14)}[fmt]
    v = np.moveaxis(np.asarray(x, np.float32).astype(ml_dtypes.bfloat16).astype(np.float64), axis, -1)
    blocks = v.reshape(v.shape[:-1] + (-1, 32))
    amax = np.abs(blocks).max(-1, keepdims=True)
    byte = np.maximum(np.where(amax > 0, np.frexp(amax)[1] - 1 + 127, 0) - down, 1)
    scale = np.exp2(byte - 127.0)
    codes = (blocks / scale).astype(np.float32).astype(dtype).astype(np.float64)
    return np.moveaxis((codes * scale).reshape(v.shape), -1, axis)


WIDE = False


def mx_kscale(k):
    if not WIDE:
        return np.ones(k)
    levels = np.array([10, -10, 5, -5, 0])
    if k % 512:
        return np.exp2(np.random.permutation(np.resize(levels, k // 32))).repeat(32)
    a = np.empty((k // 512, 16))
    for p in range(k // 512):
        a[p, :8] = np.random.permutation(np.resize(levels, 8))
        for g in range(8):
            far = levels[np.abs(levels - a[p, g]) >= 10]
            a[p, g + 8] = far[np.random.randint(len(far))]
    return np.exp2(a.ravel()).repeat(32)


BF16 = ml_dtypes.bfloat16


def bf(x):
    return np.asarray(x, np.float32).astype(BF16)


def f64(x):
    return np.asarray(x).astype(np.float64)


B, S, D, H, DH = 1, 512, 2048, 16, 128
E = H * DH
HALF = DH // 2
ROPE_BASE = 10000.0


def apply_rope(u):
    inv_freq = 1.0 / ROPE_BASE ** (np.arange(0, DH, 2) / DH)
    freqs = np.arange(S)[:, None] * inv_freq[None, :]
    cos = np.concatenate([np.cos(freqs), np.cos(freqs)], axis=-1)
    sin = np.concatenate([np.sin(freqs), np.sin(freqs)], axis=-1)
    rot = np.concatenate([-u[..., HALF:], u[..., :HALF]], axis=-1)
    return u * cos + rot * sin


def draw0():
    s = mx_kscale(D)
    return {"x": bf(np.random.standard_normal((B, S, D)) * s),
            "Wq": bf(np.random.standard_normal((E, D)) * 0.7 / np.sqrt(D) / s[None, :]),
            "Wk": bf(np.random.standard_normal((E, D)) * 0.7 / np.sqrt(D) / s[None, :])}


def core(x, Wq, Wk):
    xq = mxq(f64(x), 2, "e4m3")
    q = (xq @ mxq(f64(Wq), 1, "e4m3").T).reshape(B, S, H, DH).transpose(0, 2, 1, 3)
    k = (xq @ mxq(f64(Wk), 1, "e4m3").T).reshape(B, S, H, DH).transpose(0, 2, 1, 3)
    return apply_rope(q), apply_rope(k)


def e4m3fn_bytes(y):
    return np.clip(np.asarray(y, np.float64), -448.0, 448.0).astype(np.float32).astype(ml_dtypes.float8_e4m3fn).view(np.uint8)


def e4m3fn_values(b):
    return np.asarray(b, np.uint8).view(ml_dtypes.float8_e4m3fn).astype(np.float64)


def setup_inputs():
    d = draw0()
    x0 = np.asarray(d['Wq']).astype(np.float64)
    s = (np.max(np.abs(x0), axis=(0,), keepdims=True) / 448.0).astype(np.float32)
    out = {}
    for k, v in d.items():
        if k == 'Wq':
            out['Wq_bytes'] = e4m3fn_bytes(x0 / s.astype(np.float64))
            out['Wq_scale'] = s
        else:
            out[k] = v
    return out


def reference(x, Wq_bytes, Wq_scale, Wk):
    return core(x, e4m3fn_values(Wq_bytes) * Wq_scale.astype(np.float64), Wk)

@@ -1,0 +1,316 @@
+from contextlib import ExitStack
+import math
+
+import concourse.mybir as mybir
+from concourse.masks import make_identity
+
+S, D, H, DH = 512, 2048, 16, 128
+FLOPS = 2 * S * D * (2 * H * DH)
+
+F32 = mybir.dt.float32
+BF16 = mybir.dt.bfloat16
+I32 = mybir.dt.int32
+U32 = mybir.dt.uint32
+U8 = mybir.dt.uint8
+FP8 = mybir.dt.float8_e4m3fn
+FP8X4 = mybir.dt.float8_e4m3fn_x4
+ALU = mybir.AluOpType
+ACT = mybir.ActivationFunctionType
+ENG = mybir.EngineType
+
+P = 128
+PASSES = D // 512
+UNIT = 256
+PERIODS = (H * DH) // UNIT
+TWO_PI = 2.0 * math.pi
+TWO_PI_HI = 6.28125
+TWO_PI_LO = TWO_PI - TWO_PI_HI
+SCALAR_BANKS = (0, 1, 2, 1, 2, 1, 2, 2)
+CAST_HALVES = (3, 2, 2, 2, 2, 0, 0, 0)
+
+
+def tile_multiheadattention_pa_kernel(tc, x, Wq_bytes, Wq_scale, Wk, out_0, out_1):
+    nc = tc.nc
+    with ExitStack() as ctx:
+        const = ctx.enter_context(tc.tile_pool(name="const", bufs=1))
+        xin = ctx.enter_context(tc.tile_pool(name="xin", bufs=4))
+        xq = ctx.enter_context(tc.tile_pool(name="xq", bufs=2))
+        qbytes = ctx.enter_context(tc.tile_pool(name="qbytes", bufs=4))
+        qwide = ctx.enter_context(tc.tile_pool(name="qwide", bufs=3))
+        kin = ctx.enter_context(tc.tile_pool(name="kin", bufs=3))
+        planes = ctx.enter_context(tc.tile_pool(name="planes", bufs=3))
+        grouped = ctx.enter_context(tc.tile_pool(name="grouped", bufs=3))
+        codes = ctx.enter_context(tc.tile_pool(name="codes", bufs=4))
+        prod = ctx.enter_context(tc.tile_pool(name="prod", bufs=3))
+        res = ctx.enter_context(tc.tile_pool(name="res", bufs=3))
+        tpsum = ctx.enter_context(tc.psum_pool(name="tpsum", bufs=4))
+        mpsum = ctx.enter_context(tc.psum_pool(name="mpsum", bufs=4))
+        ctx.enter_context(tc.manual_schedule(engines={ENG.PE, ENG.DVE, ENG.Activation, ENG.Pool}))
+
+        x_rows = x.rearrange("o (a p) k -> p (o a) k", p=P)
+        q_rows = Wq_bytes.rearrange("(r p) k -> p r k", p=P)
+        k_rows = Wk.rearrange("(r p) k -> p r k", p=P)
+
+        zero = const.tile([P, 1], F32, name="zero", tag="zero")
+        warm = const.tile([P, 1], F32, name="warm", tag="warm")
+        nc.vector.memset(zero[:], 0.0)
+        nc.scalar.activation(out=warm[:], in_=zero[:], func=ACT.Sin)
+
+        ident = const.tile([P, P], F32, name="ident", tag="ident")
+        make_identity(nc, ident[:])
+
+        pos = const.tile([P, 4], F32, name="pos", tag="pos")
+        nc.gpsimd.iota(pos[:], pattern=[[P, 4]], base=0, channel_multiplier=1, allow_small_or_imprecise_dtypes=True)
+
+        q_loaded = {}
+        k_loaded = {}
+
+        def load_q(j):
+            qb = qbytes.tile([P, 2, D], U8, name="qb", tag="qb")
+            nc.sync.dma_start(out=qb[:], in_=q_rows[:, 2 * j : 2 * j + 2, :])
+            q_loaded[j] = qb
+
+        def load_k(j):
+            kb = kin.tile([P, 2, D], BF16, name="kb", tag="kb")
+            nc.sync.dma_start(out=kb[:], in_=k_rows[:, 2 * j : 2 * j + 2, :])
+            k_loaded[j] = kb
+
+        load_q(0)
+        x_sb = []
+        for a in range(4):
+            xt = xin.tile([P, D], BF16, name="xt", tag="xt")
+            nc.sync.dma_start(out=xt[:], in_=x_rows[:, a, :])
+            x_sb.append(xt)
+        sc = const.tile([P, PASSES, 4], F32, name="sc", tag="sc")
+        nc.sync.dma_start(out=sc[:], in_=Wq_scale.rearrange("o (g p t) -> p (o g) t", p=P, t=4))
+        load_k(0)
+        load_q(1)
+        load_k(1)
+        load_q(2)
+        load_k(2)
+        load_q(3)
+
+        theta = const.tile([P, 64], F32, name="theta", tag="theta")
+        nc.vector.memset(theta[:], 1.0)
+        for b in range(6):
+            step = 1 << b
+            view = theta[:].rearrange("p (hi two lo) -> p hi two lo", two=2, lo=step)[:, :, 1, :]
+            nc.vector.tensor_scalar(out=view, in0=view, scalar1=10000.0 ** (-step / 64.0), scalar2=None, op0=ALU.mult)
+        ang = const.tile([P, 2, 4, 64], F32, name="ang", tag="ang")
+        nc.vector.tensor_tensor(
+            out=ang[:, 1, :, :],
+            in0=theta[:].unsqueeze(1).to_broadcast([P, 4, 64]),
+            in1=pos[:].unsqueeze(2).to_broadcast([P, 4, 64]),
+            op=ALU.mult,
+        )
+        nc.vector.tensor_scalar(out=ang[:, 0, :, :], in0=ang[:, 1, :, :], scalar1=math.pi / 2.0, scalar2=None, op0=ALU.add)
+        ang_flat = ang[:].rearrange("p w a j -> p (w a j)")
+        turns = const.tile([P, 512], F32, name="turns", tag="turns")
+        turns_i = const.tile([P, 512], I32, name="turns_i", tag="turns_i")
+        turns_f = const.tile([P, 512], F32, name="turns_f", tag="turns_f")
+        red = const.tile([P, 512], F32, name="red", tag="red")
+        wrap = const.tile([P, 512], F32, name="wrap", tag="wrap")
+        nc.vector.tensor_scalar(out=turns[:], in0=ang_flat, scalar1=1.0 / TWO_PI, scalar2=None, op0=ALU.mult)
+        nc.vector.tensor_copy(out=turns_i[:], in_=turns[:])
+        nc.vector.tensor_copy(out=turns_f[:], in_=turns_i[:])
+        nc.vector.scalar_tensor_tensor(out=red[:], in0=turns_f[:], scalar=-TWO_PI_HI, in1=ang_flat, op0=ALU.mult, op1=ALU.add)
+        nc.vector.scalar_tensor_tensor(out=red[:], in0=turns_f[:], scalar=-TWO_PI_LO, in1=red[:], op0=ALU.mult, op1=ALU.add)
+        nc.vector.tensor_scalar(out=wrap[:], in0=red[:], scalar1=math.pi, scalar2=-TWO_PI, op0=ALU.is_gt, op1=ALU.mult)
+        nc.vector.tensor_tensor(out=red[:], in0=red[:], in1=wrap[:], op=ALU.add)
+
+        tab = const.tile([P, 2, 2, 512], F32, name="tab", tag="tab")
+
+        trig = const.tile([P, 2, 4, 64], F32, name="trig", tag="trig")
+
+        def build_tables():
+            nc.scalar.activation(out=trig[:].rearrange("p w a j -> p (w a j)"), in_=red[:], func=ACT.Sin)
+            for ap in range(2):
+                nc.gpsimd.tensor_scalar(
+                    out=tab[:, ap, 0, :].rearrange("p (a m j) -> p a m j", a=2, m=4),
+                    in0=trig[:, 0, 2 * ap : 2 * ap + 2, :].unsqueeze(2).to_broadcast([P, 2, 4, 64]),
+                    scalar1=1.0,
+                    scalar2=0.0,
+                    op0=ALU.mult,
+                    op1=ALU.add,
+                )
+                sin_v = tab[:, ap, 1, :].rearrange("p (a h f j) -> p a h f j", a=2, h=2, f=2)
+                for f in range(2):
+                    nc.gpsimd.tensor_scalar(
+                        out=sin_v[:, :, :, f, :],
+                        in0=trig[:, 1, 2 * ap : 2 * ap + 2, :].unsqueeze(2).to_broadcast([P, 2, 2, 64]),
+                        scalar1=1.0 - 2.0 * f,
+                        scalar2=0.0,
+                        op0=ALU.mult,
+                        op1=ALU.add,
+                    )
+
+        q_wide = {}
+
+        def cast_half(j, r):
+            if r == 0:
+                qf = qwide.tile([P, 2, D], BF16, name="qf", tag="qf")
+                q_wide[j] = qf
+            nc.scalar.copy(out=q_wide[j][:, r, :], in_=q_loaded[j][:, r, :].bitcast(FP8))
+
+        def turn(rows, how):
+            words = [rows[0].bitcast(F32), rows[1].bitcast(F32)]
+            wg = grouped.tile([P, PASSES, 4 * UNIT], BF16, name="wg", tag="wg", align_bytes=64)
+            waiting = []
+            for g in range(PASSES):
+                tb = tpsum.tile([P, 2 * UNIT], F32, name="tb", tag="tb")
+                for u in range(2):
+                    for r in range(2):
+                        c0 = (2 * u + r) * P
+                        nc.tensor.transpose(tb[:, c0 : c0 + P], words[r][:, 256 * g + u : 256 * (g + 1) : 2], ident[:])
+                if how[g] == "vector scaled":
+                    nc.vector.tensor_tensor(
+                        out=wg[:, g, :].rearrange("p (n u e) -> p n u e", u=2, e=2),
+                        in0=tb[:].bitcast(BF16).rearrange("p (u n e) -> p n u e", u=2, e=2),
+                        in1=sc[:, g, :].rearrange("p (u e) -> p u e", u=2).unsqueeze(1).to_broadcast([P, UNIT, 2, 2]),
+                        op=ALU.mult,
+                    )
+                elif how[g] == "scalar scaled":
+                    pl = planes.tile([P, 4, UNIT], BF16, name="pl", tag="pl")
+                    tb_v = tb[:].bitcast(BF16).rearrange("p (u n e) -> p u e n", u=2, e=2)
+                    for u in range(2):
+                        for e in range(2):
+                            t = 2 * u + e
+                            nc.scalar.activation(out=pl[:, t, :], in_=tb_v[:, u, e, :], func=ACT.Copy, scale=sc[:, g, t : t + 1])
+                    waiting.append((g, pl))
+                    if g + 1 == PASSES or how[g + 1] != "scalar scaled":
+                        for g_w, pl_w in waiting:
+                            nc.scalar.copy(
+                                out=wg[:, g_w, :].rearrange("p (n t) -> p n t", t=4), in_=pl_w[:].rearrange("p t n -> p n t")
+                            )
+                elif how[g] == "vector":
+                    nc.vector.tensor_copy(
+                        out=wg[:, g, :].bitcast(F32).rearrange("p (n u) -> p n u", u=2),
+                        in_=tb[:].rearrange("p (u n) -> p n u", u=2),
+                    )
+                else:
+                    nc.scalar.copy(
+                        out=wg[:, g, :].bitcast(F32).rearrange("p (n u) -> p n u", u=2),
+                        in_=tb[:].rearrange("p (u n) -> p n u", u=2),
+                    )
+            return wg
+
+        def quantize(wg, pool, tag):
+            wc = pool.tile([P, PASSES, UNIT], U32, name=tag + "c", tag=tag + "c", align_bytes=64)
+            ws = pool.tile([P, PASSES, UNIT], U8, name=tag + "s", tag=tag + "s", align_bytes=64)
+            nc.vector.quantize_mx(
+                out=wc[:].rearrange("p g n -> p (g n)").bitcast(FP8X4),
+                scales=ws[:].rearrange("p g n -> p (g n)"),
+                in_=wg[:].rearrange("p g c -> p (g c)"),
+            )
+            return wc, ws
+
+        x_codes = []
+
+        def turn_q(j, scalar_banks):
+            src = q_wide[j]
+            how = ["scalar scaled"] * scalar_banks + ["vector scaled"] * (PASSES - scalar_banks)
+            return turn([src[:, 0, :], src[:, 1, :]], how)
+
+        def turn_k(j):
+            src = k_loaded[j]
+            return turn([src[:, 0, :], src[:, 1, :]], ["scalar"] * PASSES)
+
+        def multiply_rotate(w_codes, ab, ap):
+            wc, ws = w_codes
+            xc, xs = x_codes[ap]
+            acc = mpsum.tile([P, 2 * UNIT], F32, name="acc", tag="acc")
+            for a2 in range(2):
+                for g in range(PASSES):
+                    nc.tensor.matmul_mx(
+                        out=acc[:, a2 * UNIT : (a2 + 1) * UNIT],
+                        lhsT=xc[:, g, a2 * P : (a2 + 1) * P].bitcast(FP8X4),
+                        lhsT_scale=xs[:, g, a2 * P : (a2 + 1) * P],
+                        rhs=wc[:, g, :].bitcast(FP8X4),
+                        rhs_scale=ws[:, g, :],
+                        start=(g == 0),
+                        stop=(g == PASSES - 1),
+                    )
+            nc.vector.tensor_tensor(
+                out=ab[:, ap, :, :],
+                in0=acc[:].unsqueeze(1).to_broadcast([P, 2, 512]),
+                in1=tab[:, ap, :, :],
+                op=ALU.mult,
+            )
+
+        def finish(ab, out, h0, last):
+            y = res.tile([P, 2, 512], F32, name="y", tag="y")
+            ab_v = ab[:].rearrange("p b w (m f j) -> p b w m f j", f=2, j=64)
+            y_v = y[:].rearrange("p b (m f j) -> p b m f j", f=2, j=64)
+            if last:
+                y_s = y[:].rearrange("p b (a h c) -> p b a h c", a=2, h=2)
+                for ap in range(2):
+                    for f in range(2):
+                        nc.vector.tensor_tensor(
+                            out=y_v[:, ap, :, f, :], in0=ab_v[:, ap, 0, :, f, :], in1=ab_v[:, ap, 1, :, 1 - f, :], op=ALU.add
+                        )
+                    for a2 in range(2):
+                        a = 2 * ap + a2
+                        nc.sync.dma_start(
+                            out=out[0, h0 : h0 + 2, a * P : (a + 1) * P, :].rearrange("h s c -> s h c"),
+                            in_=y_s[:, ap, a2, :, :],
+                        )
+            else:
+                for f in range(2):
+                    nc.gpsimd.tensor_tensor(
+                        out=y_v[:, :, :, f, :], in0=ab_v[:, :, 0, :, f, :], in1=ab_v[:, :, 1, :, 1 - f, :], op=ALU.add
+                    )
+                y_h = y[:].rearrange("p b (a h c) -> p (b a) h c", a=2, h=2)
+                for h in range(2):
+                    nc.sync.dma_start(
+                        out=out[0, h0 + h, :, :].rearrange("(a p) c -> p a c", p=P),
+                        in_=y_h[:, :, h, :],
+                    )
+
+        cast_half(0, 0)
+        cast_half(0, 1)
+        xg0 = turn([x_sb[0][:], x_sb[1][:]], ["vector"] * PASSES)
+        qg = turn_q(0, 0)
+        x_codes.append(quantize(xg0, xq, "x"))
+        build_tables()
+        cast_half(1, 0)
+        xg1 = turn([x_sb[2][:], x_sb[3][:]], ["scalar"] * PASSES)
+        q_codes = quantize(qg, codes, "w")
+        x_codes.append(quantize(xg1, xq, "x"))
+        kg = turn_k(0)
+        cast_half(1, 1)
+        k_codes = quantize(kg, codes, "w")
+        cast_half(2, 0)
+
+        halves = [(j, r) for j in range(2, PERIODS) for r in range(2)][1:]
+
+        def cast_some(first, count):
+            for j_c, r_c in halves[first : first + count]:
+                cast_half(j_c, r_c)
+
+        for j in range(PERIODS):
+            more = j + 1 < PERIODS
+            first = sum(CAST_HALVES[:j])
+            early = 0
+            if more and SCALAR_BANKS[j + 1] < 2:
+                early = min(1, CAST_HALVES[j])
+            if j + 4 < PERIODS:
+                load_q(j + 4)
+            if j + 3 < PERIODS:
+                load_k(j + 3)
+            ab_q = prod.tile([P, 2, 2, 512], F32, name="ab", tag="ab")
+            multiply_rotate(q_codes, ab_q, 0)
+            multiply_rotate(q_codes, ab_q, 1)
+            finish(ab_q, out_0, 2 * j, False)
+            if more:
+                qg = turn_q(j + 1, SCALAR_BANKS[j + 1])
+            cast_some(first, early)
+            ab_k = prod.tile([P, 2, 2, 512], F32, name="ab", tag="ab")
+            multiply_rotate(k_codes, ab_k, 0)
+            if more:
+                q_codes = quantize(qg, codes, "w")
+            multiply_rotate(k_codes, ab_k, 1)
+            if more:
+                kg = turn_k(j + 1)
+                k_codes = quantize(kg, codes, "w")
+            cast_some(first + early, CAST_HALVES[j] - early)
+            finish(ab_k, out_1, 2 * j, not more)

@@ -23,8 +23,6 @@ PASSES = D // 512
 UNIT = 256
 PERIODS = (H * DH) // UNIT
 TWO_PI = 2.0 * math.pi
-TWO_PI_HI = 6.28125
-TWO_PI_LO = TWO_PI - TWO_PI_HI
 SCALAR_BANKS = (0, 1, 2, 1, 2, 1, 2, 2)
 CAST_HALVES = (3, 2, 2, 2, 2, 0, 0, 0)
 
@@ -33,13 +31,13 @@ def tile_multiheadattention_pa_kernel(tc, x, Wq_bytes, Wq_scale, Wk, out_0, out_
     nc = tc.nc
     with ExitStack() as ctx:
         const = ctx.enter_context(tc.tile_pool(name="const", bufs=1))
-        xin = ctx.enter_context(tc.tile_pool(name="xin", bufs=4))
+        xin = ctx.enter_context(tc.tile_pool(name="xin", bufs=8))
         xq = ctx.enter_context(tc.tile_pool(name="xq", bufs=2))
         qbytes = ctx.enter_context(tc.tile_pool(name="qbytes", bufs=4))
         qwide = ctx.enter_context(tc.tile_pool(name="qwide", bufs=3))
         kin = ctx.enter_context(tc.tile_pool(name="kin", bufs=3))
         planes = ctx.enter_context(tc.tile_pool(name="planes", bufs=3))
-        grouped = ctx.enter_context(tc.tile_pool(name="grouped", bufs=3))
+        grouped = ctx.enter_context(tc.tile_pool(name="grouped", bufs=4))
         codes = ctx.enter_context(tc.tile_pool(name="codes", bufs=4))
         prod = ctx.enter_context(tc.tile_pool(name="prod", bufs=3))
         res = ctx.enter_context(tc.tile_pool(name="res", bufs=3))
@@ -56,11 +54,12 @@ def tile_multiheadattention_pa_kernel(tc, x, Wq_bytes, Wq_scale, Wk, out_0, out_
         nc.vector.memset(zero[:], 0.0)
         nc.scalar.activation(out=warm[:], in_=zero[:], func=ACT.Sin)
 
+        ang = const.tile([P, 4, 64], F32, name="ang", tag="ang")
+        ang_flat = ang[:].rearrange("p a j -> p (a j)")
+        nc.gpsimd.iota(ang_flat, pattern=[[P, 4], [0, 64]], base=0, channel_multiplier=1, allow_small_or_imprecise_dtypes=True)
+
         ident = const.tile([P, P], F32, name="ident", tag="ident")
         make_identity(nc, ident[:])
-
-        pos = const.tile([P, 4], F32, name="pos", tag="pos")
-        nc.gpsimd.iota(pos[:], pattern=[[P, 4]], base=0, channel_multiplier=1, allow_small_or_imprecise_dtypes=True)
 
         q_loaded = {}
         k_loaded = {}
@@ -76,13 +75,15 @@ def tile_multiheadattention_pa_kernel(tc, x, Wq_bytes, Wq_scale, Wk, out_0, out_
             k_loaded[j] = kb
 
         load_q(0)
-        x_sb = []
-        for a in range(4):
-            xt = xin.tile([P, D], BF16, name="xt", tag="xt")
-            nc.sync.dma_start(out=xt[:], in_=x_rows[:, a, :])
-            x_sb.append(xt)
+        x_sb = {}
         sc = const.tile([P, PASSES, 4], F32, name="sc", tag="sc")
-        nc.sync.dma_start(out=sc[:], in_=Wq_scale.rearrange("o (g p t) -> p (o g) t", p=P, t=4))
+        for ap in range(2):
+            for g in range(PASSES):
+                xt = xin.tile([P, 2, 512], BF16, name="xt", tag="xt")
+                nc.sync.dma_start(out=xt[:], in_=x_rows[:, 2 * ap : 2 * ap + 2, 512 * g : 512 * (g + 1)])
+                x_sb[(ap, g)] = xt
+            if ap == 0:
+                nc.sync.dma_start(out=sc[:], in_=Wq_scale.rearrange("o (g p t) -> p (o g) t", p=P, t=4))
         load_k(0)
         load_q(1)
         load_k(1)
@@ -90,40 +91,25 @@ def tile_multiheadattention_pa_kernel(tc, x, Wq_bytes, Wq_scale, Wk, out_0, out_
         load_k(2)
         load_q(3)
 
-        theta = const.tile([P, 64], F32, name="theta", tag="theta")
-        nc.vector.memset(theta[:], 1.0)
         for b in range(6):
             step = 1 << b
-            view = theta[:].rearrange("p (hi two lo) -> p hi two lo", two=2, lo=step)[:, :, 1, :]
+            view = ang_flat.rearrange("p (hi two lo) -> p hi two lo", two=2, lo=step)[:, :, 1, :]
             nc.vector.tensor_scalar(out=view, in0=view, scalar1=10000.0 ** (-step / 64.0), scalar2=None, op0=ALU.mult)
-        ang = const.tile([P, 2, 4, 64], F32, name="ang", tag="ang")
-        nc.vector.tensor_tensor(
-            out=ang[:, 1, :, :],
-            in0=theta[:].unsqueeze(1).to_broadcast([P, 4, 64]),
-            in1=pos[:].unsqueeze(2).to_broadcast([P, 4, 64]),
-            op=ALU.mult,
-        )
-        nc.vector.tensor_scalar(out=ang[:, 0, :, :], in0=ang[:, 1, :, :], scalar1=math.pi / 2.0, scalar2=None, op0=ALU.add)
-        ang_flat = ang[:].rearrange("p w a j -> p (w a j)")
-        turns = const.tile([P, 512], F32, name="turns", tag="turns")
-        turns_i = const.tile([P, 512], I32, name="turns_i", tag="turns_i")
-        turns_f = const.tile([P, 512], F32, name="turns_f", tag="turns_f")
-        red = const.tile([P, 512], F32, name="red", tag="red")
-        wrap = const.tile([P, 512], F32, name="wrap", tag="wrap")
-        nc.vector.tensor_scalar(out=turns[:], in0=ang_flat, scalar1=1.0 / TWO_PI, scalar2=None, op0=ALU.mult)
-        nc.vector.tensor_copy(out=turns_i[:], in_=turns[:])
-        nc.vector.tensor_copy(out=turns_f[:], in_=turns_i[:])
-        nc.vector.scalar_tensor_tensor(out=red[:], in0=turns_f[:], scalar=-TWO_PI_HI, in1=ang_flat, op0=ALU.mult, op1=ALU.add)
-        nc.vector.scalar_tensor_tensor(out=red[:], in0=turns_f[:], scalar=-TWO_PI_LO, in1=red[:], op0=ALU.mult, op1=ALU.add)
-        nc.vector.tensor_scalar(out=wrap[:], in0=red[:], scalar1=math.pi, scalar2=-TWO_PI, op0=ALU.is_gt, op1=ALU.mult)
-        nc.vector.tensor_tensor(out=red[:], in0=red[:], in1=wrap[:], op=ALU.add)
+        turns_i = const.tile([P, 256], I32, name="turns_i", tag="turns_i")
+        red = const.tile([P, 2, 256], F32, name="red", tag="red")
+        down = const.tile([P, 256], F32, name="down", tag="down")
+        red_s = red[:, 1, :]
+        nc.vector.tensor_scalar(out=turns_i[:], in0=ang_flat, scalar1=1.0 / TWO_PI, scalar2=None, op0=ALU.mult)
+        nc.vector.scalar_tensor_tensor(out=red_s, in0=turns_i[:], scalar=-TWO_PI, in1=ang_flat, op0=ALU.mult, op1=ALU.add)
+        nc.vector.tensor_scalar(out=down[:], in0=red_s, scalar1=-1.0, scalar2=math.pi / 2.0, op0=ALU.mult, op1=ALU.add)
+        nc.vector.scalar_tensor_tensor(out=red[:, 0, :], in0=red_s, scalar=math.pi / 2.0, in1=down[:], op0=ALU.add, op1=ALU.min)
 
         tab = const.tile([P, 2, 2, 512], F32, name="tab", tag="tab")
 
         trig = const.tile([P, 2, 4, 64], F32, name="trig", tag="trig")
 
         def build_tables():
-            nc.scalar.activation(out=trig[:].rearrange("p w a j -> p (w a j)"), in_=red[:], func=ACT.Sin)
+            nc.scalar.activation(out=trig[:].rearrange("p w a j -> p (w a j)"), in_=red[:].rearrange("p w c -> p (w c)"), func=ACT.Sin)
             for ap in range(2):
                 nc.gpsimd.tensor_scalar(
                     out=tab[:, ap, 0, :].rearrange("p (a m j) -> p a m j", a=2, m=4),
@@ -152,16 +138,26 @@ def tile_multiheadattention_pa_kernel(tc, x, Wq_bytes, Wq_scale, Wk, out_0, out_
                 q_wide[j] = qf
             nc.scalar.copy(out=q_wide[j][:, r, :], in_=q_loaded[j][:, r, :].bitcast(FP8))
 
-        def turn(rows, how):
-            words = [rows[0].bitcast(F32), rows[1].bitcast(F32)]
+        def cast_first_unit():
+            qf = qwide.tile([P, 2, D], BF16, name="qf", tag="qf")
+            q_wide[0] = qf
+            for c in range(2):
+                for r in range(2):
+                    cols = slice(c * (D // 2), (c + 1) * (D // 2))
+                    nc.scalar.copy(out=qf[:, r, cols], in_=q_loaded[0][:, r, cols].bitcast(FP8))
+
+        def turn(rows, how, in_product_banks=False):
             wg = grouped.tile([P, PASSES, 4 * UNIT], BF16, name="wg", tag="wg", align_bytes=64)
             waiting = []
             for g in range(PASSES):
-                tb = tpsum.tile([P, 2 * UNIT], F32, name="tb", tag="tb")
+                if in_product_banks:
+                    tb = mpsum.tile([P, 2 * UNIT], F32, name="acc", tag="acc")
+                else:
+                    tb = tpsum.tile([P, 2 * UNIT], F32, name="tb", tag="tb")
                 for u in range(2):
                     for r in range(2):
                         c0 = (2 * u + r) * P
-                        nc.tensor.transpose(tb[:, c0 : c0 + P], words[r][:, 256 * g + u : 256 * (g + 1) : 2], ident[:])
+                        nc.tensor.transpose(tb[:, c0 : c0 + P], rows(r, g)[:, u:256:2], ident[:])
                 if how[g] == "vector scaled":
                     nc.vector.tensor_tensor(
                         out=wg[:, g, :].rearrange("p (n u e) -> p n u e", u=2, e=2),
@@ -209,11 +205,14 @@ def tile_multiheadattention_pa_kernel(tc, x, Wq_bytes, Wq_scale, Wk, out_0, out_
         def turn_q(j, scalar_banks):
             src = q_wide[j]
             how = ["scalar scaled"] * scalar_banks + ["vector scaled"] * (PASSES - scalar_banks)
-            return turn([src[:, 0, :], src[:, 1, :]], how)
+            return turn(lambda r, g: src[:, r, 512 * g : 512 * (g + 1)].bitcast(F32), how)
 
         def turn_k(j):
             src = k_loaded[j]
-            return turn([src[:, 0, :], src[:, 1, :]], ["scalar"] * PASSES)
+            return turn(lambda r, g: src[:, r, 512 * g : 512 * (g + 1)].bitcast(F32), ["scalar"] * PASSES)
+
+        def turn_x(ap, engine):
+            return turn(lambda r, g: x_sb[(ap, g)][:, r, :].bitcast(F32), [engine] * PASSES, in_product_banks=(ap == 1))
 
         def multiply_rotate(w_codes, ab, ap):
             wc, ws = w_codes
@@ -266,19 +265,18 @@ def tile_multiheadattention_pa_kernel(tc, x, Wq_bytes, Wq_scale, Wk, out_0, out_
                         in_=y_h[:, :, h, :],
                     )
 
-        cast_half(0, 0)
-        cast_half(0, 1)
-        xg0 = turn([x_sb[0][:], x_sb[1][:]], ["vector"] * PASSES)
+        cast_first_unit()
+        xg0 = turn_x(0, "vector")
         qg = turn_q(0, 0)
         x_codes.append(quantize(xg0, xq, "x"))
         build_tables()
-        cast_half(1, 0)
-        xg1 = turn([x_sb[2][:], x_sb[3][:]], ["scalar"] * PASSES)
+        xg1 = turn_x(1, "scalar")
         q_codes = quantize(qg, codes, "w")
         x_codes.append(quantize(xg1, xq, "x"))
         kg = turn_k(0)
-        cast_half(1, 1)
         k_codes = quantize(kg, codes, "w")
+        cast_half(1, 0)
+        cast_half(1, 1)
         cast_half(2, 0)
 
         halves = [(j, r) for j in range(2, PERIODS) for r in range(2)][1:]

@@ -24,7 +24,7 @@ UNIT = 256
 PERIODS = (H * DH) // UNIT
 TWO_PI = 2.0 * math.pi
 SCALAR_BANKS = (0, 1, 2, 1, 2, 1, 2, 2)
-CAST_HALVES = (3, 2, 2, 2, 2, 0, 0, 0)
+CAST_HALVES = (2, 2, 2, 2, 2, 1, 0, 0)
 
 
 def tile_multiheadattention_pa_kernel(tc, x, Wq_bytes, Wq_scale, Wk, out_0, out_1):

@@ -45,7 +45,7 @@ def tile_multiheadattention_pa_kernel(tc, x, Wq_bytes, Wq_scale, Wk, out_0, out_
         mpsum = ctx.enter_context(tc.psum_pool(name="mpsum", bufs=4))
         ctx.enter_context(tc.manual_schedule(engines={ENG.PE, ENG.DVE, ENG.Activation, ENG.Pool}))
 
-        x_rows = x.rearrange("o (a p) k -> p (o a) k", p=P)
+        x_rows = x.rearrange("o (p a) k -> p (o a) k", a=4)
         q_rows = Wq_bytes.rearrange("(r p) k -> p r k", p=P)
         k_rows = Wk.rearrange("(r p) k -> p r k", p=P)
 
@@ -56,7 +56,7 @@ def tile_multiheadattention_pa_kernel(tc, x, Wq_bytes, Wq_scale, Wk, out_0, out_
 
         ang = const.tile([P, 4, 64], F32, name="ang", tag="ang")
         ang_flat = ang[:].rearrange("p a j -> p (a j)")
-        nc.gpsimd.iota(ang_flat, pattern=[[P, 4], [0, 64]], base=0, channel_multiplier=1, allow_small_or_imprecise_dtypes=True)
+        nc.gpsimd.iota(ang_flat, pattern=[[1, 4], [0, 64]], base=0, channel_multiplier=4, allow_small_or_imprecise_dtypes=True)
 
         ident = const.tile([P, P], F32, name="ident", tag="ident")
         make_identity(nc, ident[:])
@@ -230,40 +230,31 @@ def tile_multiheadattention_pa_kernel(tc, x, Wq_bytes, Wq_scale, Wk, out_0, out_
                         stop=(g == PASSES - 1),
                     )
             nc.vector.tensor_tensor(
-                out=ab[:, ap, :, :],
+                out=ab[:, :, ap, :],
                 in0=acc[:].unsqueeze(1).to_broadcast([P, 2, 512]),
                 in1=tab[:, ap, :, :],
                 op=ALU.mult,
             )
 
         def finish(ab, out, h0, last):
-            y = res.tile([P, 2, 512], F32, name="y", tag="y")
-            ab_v = ab[:].rearrange("p b w (m f j) -> p b w m f j", f=2, j=64)
-            y_v = y[:].rearrange("p b (m f j) -> p b m f j", f=2, j=64)
+            y = res.tile([P, 2, 4, DH], F32, name="y", tag="y")
+            ab_v = ab[:].rearrange("p w b (a h f j) -> p w h (b a) f j", a=2, h=2, f=2)
+            y_v = y[:].rearrange("p h a (f j) -> p h a f j", f=2)
+            out_v = out[0, h0 : h0 + 2, :, :].rearrange("h (p a) c -> p h a c", a=4)
             if last:
-                y_s = y[:].rearrange("p b (a h c) -> p b a h c", a=2, h=2)
                 for ap in range(2):
+                    rows = slice(2 * ap, 2 * ap + 2)
                     for f in range(2):
                         nc.vector.tensor_tensor(
-                            out=y_v[:, ap, :, f, :], in0=ab_v[:, ap, 0, :, f, :], in1=ab_v[:, ap, 1, :, 1 - f, :], op=ALU.add
+                            out=y_v[:, :, rows, f, :], in0=ab_v[:, 0, :, rows, f, :], in1=ab_v[:, 1, :, rows, 1 - f, :], op=ALU.add
                         )
-                    for a2 in range(2):
-                        a = 2 * ap + a2
-                        nc.sync.dma_start(
-                            out=out[0, h0 : h0 + 2, a * P : (a + 1) * P, :].rearrange("h s c -> s h c"),
-                            in_=y_s[:, ap, a2, :, :],
-                        )
+                    nc.sync.dma_start(out=out_v[:, :, rows, :], in_=y[:, :, rows, :])
             else:
                 for f in range(2):
                     nc.gpsimd.tensor_tensor(
-                        out=y_v[:, :, :, f, :], in0=ab_v[:, :, 0, :, f, :], in1=ab_v[:, :, 1, :, 1 - f, :], op=ALU.add
+                        out=y_v[:, :, :, f, :], in0=ab_v[:, 0, :, :, f, :], in1=ab_v[:, 1, :, :, 1 - f, :], op=ALU.add
                     )
-                y_h = y[:].rearrange("p b (a h c) -> p (b a) h c", a=2, h=2)
-                for h in range(2):
-                    nc.sync.dma_start(
-                        out=out[0, h0 + h, :, :].rearrange("(a p) c -> p a c", p=P),
-                        in_=y_h[:, :, h, :],
-                    )
+                nc.sync.dma_start(out=out_v, in_=y[:])
 
         cast_first_unit()
         xg0 = turn_x(0, "vector")

@@ -236,16 +236,16 @@ def tile_multiheadattention_pa_kernel(tc, x, Wq_bytes, Wq_scale, Wk, out_0, out_
                 op=ALU.mult,
             )
 
-        def finish(ab, out, h0, last):
+        def finish(ab, out, h0, halves_on):
             y = res.tile([P, 2, 4, DH], F32, name="y", tag="y")
             ab_v = ab[:].rearrange("p w b (a h f j) -> p w h (b a) f j", a=2, h=2, f=2)
             y_v = y[:].rearrange("p h a (f j) -> p h a f j", f=2)
             out_v = out[0, h0 : h0 + 2, :, :].rearrange("h (p a) c -> p h a c", a=4)
-            if last:
+            if halves_on is not None:
                 for ap in range(2):
                     rows = slice(2 * ap, 2 * ap + 2)
                     for f in range(2):
-                        nc.vector.tensor_tensor(
+                        halves_on.tensor_tensor(
                             out=y_v[:, :, rows, f, :], in0=ab_v[:, 0, :, rows, f, :], in1=ab_v[:, 1, :, rows, 1 - f, :], op=ALU.add
                         )
                     nc.sync.dma_start(out=out_v[:, :, rows, :], in_=y[:, :, rows, :])
@@ -289,7 +289,7 @@ def tile_multiheadattention_pa_kernel(tc, x, Wq_bytes, Wq_scale, Wk, out_0, out_
             ab_q = prod.tile([P, 2, 2, 512], F32, name="ab", tag="ab")
             multiply_rotate(q_codes, ab_q, 0)
             multiply_rotate(q_codes, ab_q, 1)
-            finish(ab_q, out_0, 2 * j, False)
+            finish(ab_q, out_0, 2 * j, None if more else nc.gpsimd)
             if more:
                 qg = turn_q(j + 1, SCALAR_BANKS[j + 1])
             cast_some(first, early)
@@ -302,4 +302,4 @@ def tile_multiheadattention_pa_kernel(tc, x, Wq_bytes, Wq_scale, Wk, out_0, out_
                 kg = turn_k(j + 1)
                 k_codes = quantize(kg, codes, "w")
             cast_some(first + early, CAST_HALVES[j] - early)
-            finish(ab_k, out_1, 2 * j, not more)
+            finish(ab_k, out_1, 2 * j, None if more else nc.vector)

@@ -82,8 +82,8 @@ def tile_multiheadattention_pa_kernel(tc, x, Wq_bytes, Wq_scale, Wk, out_0, out_
                 xt = xin.tile([P, 2, 512], BF16, name="xt", tag="xt")
                 nc.sync.dma_start(out=xt[:], in_=x_rows[:, 2 * ap : 2 * ap + 2, 512 * g : 512 * (g + 1)])
                 x_sb[(ap, g)] = xt
-            if ap == 0:
-                nc.sync.dma_start(out=sc[:], in_=Wq_scale.rearrange("o (g p t) -> p (o g) t", p=P, t=4))
+                if ap == 0 and g == 1:
+                    nc.sync.dma_start(out=sc[:], in_=Wq_scale.rearrange("o (g p t) -> p (o g) t", p=P, t=4))
         load_k(0)
         load_q(1)
         load_k(1)
@@ -99,10 +99,12 @@ def tile_multiheadattention_pa_kernel(tc, x, Wq_bytes, Wq_scale, Wk, out_0, out_
         red = const.tile([P, 2, 256], F32, name="red", tag="red")
         down = const.tile([P, 256], F32, name="down", tag="down")
         red_s = red[:, 1, :]
-        nc.vector.tensor_scalar(out=turns_i[:], in0=ang_flat, scalar1=1.0 / TWO_PI, scalar2=None, op0=ALU.mult)
-        nc.vector.scalar_tensor_tensor(out=red_s, in0=turns_i[:], scalar=-TWO_PI, in1=ang_flat, op0=ALU.mult, op1=ALU.add)
-        nc.vector.tensor_scalar(out=down[:], in0=red_s, scalar1=-1.0, scalar2=math.pi / 2.0, op0=ALU.mult, op1=ALU.add)
-        nc.vector.scalar_tensor_tensor(out=red[:, 0, :], in0=red_s, scalar=math.pi / 2.0, in1=down[:], op0=ALU.add, op1=ALU.min)
+
+        def reduce_angles():
+            nc.vector.tensor_scalar(out=turns_i[:], in0=ang_flat, scalar1=1.0 / TWO_PI, scalar2=None, op0=ALU.mult)
+            nc.vector.scalar_tensor_tensor(out=red_s, in0=turns_i[:], scalar=-TWO_PI, in1=ang_flat, op0=ALU.mult, op1=ALU.add)
+            nc.vector.tensor_scalar(out=down[:], in0=red_s, scalar1=-1.0, scalar2=math.pi / 2.0, op0=ALU.mult, op1=ALU.add)
+            nc.vector.scalar_tensor_tensor(out=red[:, 0, :], in0=red_s, scalar=math.pi / 2.0, in1=down[:], op0=ALU.add, op1=ALU.min)
 
         tab = const.tile([P, 2, 2, 512], F32, name="tab", tag="tab")
 
@@ -141,15 +143,16 @@ def tile_multiheadattention_pa_kernel(tc, x, Wq_bytes, Wq_scale, Wk, out_0, out_
         def cast_first_unit():
             qf = qwide.tile([P, 2, D], BF16, name="qf", tag="qf")
             q_wide[0] = qf
-            for c in range(2):
-                for r in range(2):
-                    cols = slice(c * (D // 2), (c + 1) * (D // 2))
-                    nc.scalar.copy(out=qf[:, r, cols], in_=q_loaded[0][:, r, cols].bitcast(FP8))
+            for r in range(2):
+                nc.scalar.copy(out=qf[:, r, 0 : D // 2], in_=q_loaded[0][:, r, 0 : D // 2].bitcast(FP8))
+            for r in range(2):
+                nc.vector.tensor_copy(out=qf[:, r, D // 2 : D], in_=q_loaded[0][:, r, D // 2 : D].bitcast(FP8))
 
-        def turn(rows, how, in_product_banks=False):
-            wg = grouped.tile([P, PASSES, 4 * UNIT], BF16, name="wg", tag="wg", align_bytes=64)
+        def turn(rows, how, in_product_banks=False, wg=None, passes=(0, 1, 2, 3)):
+            if wg is None:
+                wg = grouped.tile([P, PASSES, 4 * UNIT], BF16, name="wg", tag="wg", align_bytes=64)
             waiting = []
-            for g in range(PASSES):
+            for g in passes:
                 if in_product_banks:
                     tb = mpsum.tile([P, 2 * UNIT], F32, name="acc", tag="acc")
                 else:
@@ -202,17 +205,19 @@ def tile_multiheadattention_pa_kernel(tc, x, Wq_bytes, Wq_scale, Wk, out_0, out_
 
         x_codes = []
 
-        def turn_q(j, scalar_banks):
+        def turn_q(j, scalar_banks, wg=None, passes=(0, 1, 2, 3)):
             src = q_wide[j]
             how = ["scalar scaled"] * scalar_banks + ["vector scaled"] * (PASSES - scalar_banks)
-            return turn(lambda r, g: src[:, r, 512 * g : 512 * (g + 1)].bitcast(F32), how)
+            return turn(lambda r, g: src[:, r, 512 * g : 512 * (g + 1)].bitcast(F32), how, wg=wg, passes=passes)
 
         def turn_k(j):
             src = k_loaded[j]
             return turn(lambda r, g: src[:, r, 512 * g : 512 * (g + 1)].bitcast(F32), ["scalar"] * PASSES)
 
-        def turn_x(ap, engine):
-            return turn(lambda r, g: x_sb[(ap, g)][:, r, :].bitcast(F32), [engine] * PASSES, in_product_banks=(ap == 1))
+        def turn_x(ap, wg=None, passes=(0, 1, 2, 3)):
+            return turn(
+                lambda r, g: x_sb[(ap, g)][:, r, :].bitcast(F32), ["scalar"] * PASSES, in_product_banks=True, wg=wg, passes=passes
+            )
 
         def multiply_rotate(w_codes, ab, ap):
             wc, ws = w_codes
@@ -257,12 +262,15 @@ def tile_multiheadattention_pa_kernel(tc, x, Wq_bytes, Wq_scale, Wk, out_0, out_
                 nc.sync.dma_start(out=out_v, in_=y[:])
 
         cast_first_unit()
-        xg0 = turn_x(0, "vector")
-        qg = turn_q(0, 0)
-        x_codes.append(quantize(xg0, xq, "x"))
-        build_tables()
-        xg1 = turn_x(1, "scalar")
+        reduce_angles()
+        xg0 = turn_x(0, passes=(0, 1))
+        qg = turn_q(0, 0, passes=(2, 3))
+        turn_x(0, wg=xg0, passes=(2, 3))
+        turn_q(0, 0, wg=qg, passes=(0, 1))
         q_codes = quantize(qg, codes, "w")
+        build_tables()
+        x_codes.append(quantize(xg0, xq, "x"))
+        xg1 = turn_x(1)
         x_codes.append(quantize(xg1, xq, "x"))
         kg = turn_k(0)
         k_codes = quantize(kg, codes, "w")

@@ -210,9 +210,9 @@ def tile_multiheadattention_pa_kernel(tc, x, Wq_bytes, Wq_scale, Wk, out_0, out_
             how = ["scalar scaled"] * scalar_banks + ["vector scaled"] * (PASSES - scalar_banks)
             return turn(lambda r, g: src[:, r, 512 * g : 512 * (g + 1)].bitcast(F32), how, wg=wg, passes=passes)
 
-        def turn_k(j):
+        def turn_k(j, wg=None, passes=(0, 1, 2, 3)):
             src = k_loaded[j]
-            return turn(lambda r, g: src[:, r, 512 * g : 512 * (g + 1)].bitcast(F32), ["scalar"] * PASSES)
+            return turn(lambda r, g: src[:, r, 512 * g : 512 * (g + 1)].bitcast(F32), ["scalar"] * PASSES, wg=wg, passes=passes)
 
         def turn_x(ap, wg=None, passes=(0, 1, 2, 3)):
             return turn(
@@ -296,18 +296,21 @@ def tile_multiheadattention_pa_kernel(tc, x, Wq_bytes, Wq_scale, Wk, out_0, out_
                 load_k(j + 3)
             ab_q = prod.tile([P, 2, 2, 512], F32, name="ab", tag="ab")
             multiply_rotate(q_codes, ab_q, 0)
+            if more:
+                qg = turn_q(j + 1, SCALAR_BANKS[j + 1], passes=(0, 1))
             multiply_rotate(q_codes, ab_q, 1)
             finish(ab_q, out_0, 2 * j, None if more else nc.gpsimd)
             if more:
-                qg = turn_q(j + 1, SCALAR_BANKS[j + 1])
+                turn_q(j + 1, SCALAR_BANKS[j + 1], wg=qg, passes=(2, 3))
             cast_some(first, early)
             ab_k = prod.tile([P, 2, 2, 512], F32, name="ab", tag="ab")
             multiply_rotate(k_codes, ab_k, 0)
             if more:
+                kg = turn_k(j + 1, passes=(0, 1))
                 q_codes = quantize(qg, codes, "w")
             multiply_rotate(k_codes, ab_k, 1)
             if more:
-                kg = turn_k(j + 1)
+                turn_k(j + 1, wg=kg, passes=(2, 3))
                 k_codes = quantize(kg, codes, "w")
             cast_some(first + early, CAST_HALVES[j] - early)
             finish(ab_k, out_1, 2 * j, None if more else nc.vector)

@@ -22,6 +22,7 @@ P = 128
 PASSES = D // 512
 UNIT = 256
 PERIODS = (H * DH) // UNIT
+TURNED_BY_MATMUL = range(1, 7)
 TWO_PI = 2.0 * math.pi
 SCALAR_BANKS = (0, 1, 2, 1, 2, 1, 2, 2)
 CAST_HALVES = (2, 2, 2, 2, 2, 1, 0, 0)
@@ -60,6 +61,8 @@ def tile_multiheadattention_pa_kernel(tc, x, Wq_bytes, Wq_scale, Wk, out_0, out_
 
         ident = const.tile([P, P], F32, name="ident", tag="ident")
         make_identity(nc, ident[:])
+        ident_b = const.tile([P, P], BF16, name="ident_b", tag="ident_b")
+        make_identity(nc, ident_b[:])
 
         q_loaded = {}
         k_loaded = {}
@@ -205,7 +208,44 @@ def tile_multiheadattention_pa_kernel(tc, x, Wq_bytes, Wq_scale, Wk, out_0, out_
 
         x_codes = []
 
+        def turn_by_matmul(j, scalar_banks, wg, passes):
+            if wg is None:
+                wg = grouped.tile([P, PASSES, 4 * UNIT], BF16, name="wg", tag="wg", align_bytes=64)
+            waiting = []
+            for g in passes:
+                tb = tpsum.tile([P, 4, UNIT], BF16, name="tb", tag="tb")
+                for r in range(2):
+                    for t in range(4):
+                        nc.tensor.matmul(
+                            out=tb[:, t, r * P : (r + 1) * P],
+                            lhsT=q_wide[j][:, r, 512 * g + t : 512 * (g + 1) : 4],
+                            rhs=ident_b[:],
+                            start=True,
+                            stop=True,
+                        )
+                if g < scalar_banks:
+                    pl = planes.tile([P, 4, UNIT], BF16, name="pl", tag="pl")
+                    for t in range(4):
+                        nc.scalar.activation(out=pl[:, t, :], in_=tb[:, t, :], func=ACT.Copy, scale=sc[:, g, t : t + 1])
+                    waiting.append((g, pl))
+                    if g == passes[-1] or g + 1 == scalar_banks:
+                        for g_w, pl_w in waiting:
+                            nc.scalar.copy(
+                                out=wg[:, g_w, :].rearrange("p (n t) -> p n t", t=4), in_=pl_w[:].rearrange("p t n -> p n t")
+                            )
+                        waiting = []
+                else:
+                    nc.vector.tensor_tensor(
+                        out=wg[:, g, :].rearrange("p (n t) -> p n t", t=4),
+                        in0=tb[:].rearrange("p t n -> p n t"),
+                        in1=sc[:, g, :].unsqueeze(1).to_broadcast([P, UNIT, 4]),
+                        op=ALU.mult,
+                    )
+            return wg
+
         def turn_q(j, scalar_banks, wg=None, passes=(0, 1, 2, 3)):
+            if j in TURNED_BY_MATMUL:
+                return turn_by_matmul(j, scalar_banks, wg, passes)
             src = q_wide[j]
             how = ["scalar scaled"] * scalar_banks + ["vector scaled"] * (PASSES - scalar_banks)
             return turn(lambda r, g: src[:, r, 512 * g : 512 * (g + 1)].bitcast(F32), how, wg=wg, passes=passes)

@@ -24,8 +24,7 @@ UNIT = 256
 PERIODS = (H * DH) // UNIT
 TURNED_BY_MATMUL = range(1, 7)
 TWO_PI = 2.0 * math.pi
-SCALAR_BANKS = (0, 1, 2, 1, 2, 1, 2, 2)
-CAST_HALVES = (2, 2, 2, 2, 2, 1, 0, 0)
+SCALAR_BANKS = (0, 1, 2, 2, 2, 2, 2, 2)
 
 
 def tile_multiheadattention_pa_kernel(tc, x, Wq_bytes, Wq_scale, Wk, out_0, out_1):
@@ -318,18 +317,8 @@ def tile_multiheadattention_pa_kernel(tc, x, Wq_bytes, Wq_scale, Wk, out_0, out_
         cast_half(1, 1)
         cast_half(2, 0)
 
-        halves = [(j, r) for j in range(2, PERIODS) for r in range(2)][1:]
-
-        def cast_some(first, count):
-            for j_c, r_c in halves[first : first + count]:
-                cast_half(j_c, r_c)
-
         for j in range(PERIODS):
             more = j + 1 < PERIODS
-            first = sum(CAST_HALVES[:j])
-            early = 0
-            if more and SCALAR_BANKS[j + 1] < 2:
-                early = min(1, CAST_HALVES[j])
             if j + 4 < PERIODS:
                 load_q(j + 4)
             if j + 3 < PERIODS:
@@ -342,7 +331,8 @@ def tile_multiheadattention_pa_kernel(tc, x, Wq_bytes, Wq_scale, Wk, out_0, out_
             finish(ab_q, out_0, 2 * j, None if more else nc.gpsimd)
             if more:
                 turn_q(j + 1, SCALAR_BANKS[j + 1], wg=qg, passes=(2, 3))
-            cast_some(first, early)
+            if j + 2 < PERIODS:
+                cast_half(j + 2, 1)
             ab_k = prod.tile([P, 2, 2, 512], F32, name="ab", tag="ab")
             multiply_rotate(k_codes, ab_k, 0)
             if more:
@@ -352,5 +342,6 @@ def tile_multiheadattention_pa_kernel(tc, x, Wq_bytes, Wq_scale, Wk, out_0, out_
             if more:
                 turn_k(j + 1, wg=kg, passes=(2, 3))
                 k_codes = quantize(kg, codes, "w")
-            cast_some(first + early, CAST_HALVES[j] - early)
+            if j + 3 < PERIODS:
+                cast_half(j + 3, 0)
             finish(ab_k, out_1, 2 * j, None if more else nc.vector)

@@ -58,21 +58,21 @@ def tile_multiheadattention_pa_kernel(tc, x, Wq_bytes, Wq_scale, Wk, out_0, out_
         ang_flat = ang[:].rearrange("p a j -> p (a j)")
         nc.gpsimd.iota(ang_flat, pattern=[[1, 4], [0, 64]], base=0, channel_multiplier=4, allow_small_or_imprecise_dtypes=True)
 
-        ident = const.tile([P, P], F32, name="ident", tag="ident")
+        ident = const.tile([P, P], F32, name="ident", tag="ident", align_bytes=256)
         make_identity(nc, ident[:])
-        ident_b = const.tile([P, P], BF16, name="ident_b", tag="ident_b")
+        ident_b = const.tile([P, P], BF16, name="ident_b", tag="ident_b", align_bytes=256)
         make_identity(nc, ident_b[:])
 
         q_loaded = {}
         k_loaded = {}
 
         def load_q(j):
-            qb = qbytes.tile([P, 2, D], U8, name="qb", tag="qb")
+            qb = qbytes.tile([P, 2, D], U8, name="qb", tag="qb", align_bytes=256)
             nc.sync.dma_start(out=qb[:], in_=q_rows[:, 2 * j : 2 * j + 2, :])
             q_loaded[j] = qb
 
         def load_k(j):
-            kb = kin.tile([P, 2, D], BF16, name="kb", tag="kb")
+            kb = kin.tile([P, 2, D], BF16, name="kb", tag="kb", align_bytes=256)
             nc.sync.dma_start(out=kb[:], in_=k_rows[:, 2 * j : 2 * j + 2, :])
             k_loaded[j] = kb
 
@@ -81,7 +81,7 @@ def tile_multiheadattention_pa_kernel(tc, x, Wq_bytes, Wq_scale, Wk, out_0, out_
         sc = const.tile([P, PASSES, 4], F32, name="sc", tag="sc")
         for ap in range(2):
             for g in range(PASSES):
-                xt = xin.tile([P, 2, 512], BF16, name="xt", tag="xt")
+                xt = xin.tile([P, 2, 512], BF16, name="xt", tag="xt", align_bytes=256)
                 nc.sync.dma_start(out=xt[:], in_=x_rows[:, 2 * ap : 2 * ap + 2, 512 * g : 512 * (g + 1)])
                 x_sb[(ap, g)] = xt
                 if ap == 0 and g == 1:
@@ -108,7 +108,7 @@ def tile_multiheadattention_pa_kernel(tc, x, Wq_bytes, Wq_scale, Wk, out_0, out_
             nc.vector.tensor_scalar(out=down[:], in0=red_s, scalar1=-1.0, scalar2=math.pi / 2.0, op0=ALU.mult, op1=ALU.add)
             nc.vector.scalar_tensor_tensor(out=red[:, 0, :], in0=red_s, scalar=math.pi / 2.0, in1=down[:], op0=ALU.add, op1=ALU.min)
 
-        tab = const.tile([P, 2, 2, 512], F32, name="tab", tag="tab")
+        tab = const.tile([P, 2, 2, 512], F32, name="tab", tag="tab", align_bytes=256)
 
         trig = const.tile([P, 2, 4, 64], F32, name="trig", tag="trig")
 
@@ -138,12 +138,12 @@ def tile_multiheadattention_pa_kernel(tc, x, Wq_bytes, Wq_scale, Wk, out_0, out_
 
         def cast_half(j, r):
             if r == 0:
-                qf = qwide.tile([P, 2, D], BF16, name="qf", tag="qf")
+                qf = qwide.tile([P, 2, D], BF16, name="qf", tag="qf", align_bytes=256)
                 q_wide[j] = qf
             nc.scalar.copy(out=q_wide[j][:, r, :], in_=q_loaded[j][:, r, :].bitcast(FP8))
 
         def cast_first_unit():
-            qf = qwide.tile([P, 2, D], BF16, name="qf", tag="qf")
+            qf = qwide.tile([P, 2, D], BF16, name="qf", tag="qf", align_bytes=256)
             q_wide[0] = qf
             for r in range(2):
                 nc.scalar.copy(out=qf[:, r, 0 : D // 2], in_=q_loaded[0][:, r, 0 : D // 2].bitcast(FP8))
@@ -152,7 +152,7 @@ def tile_multiheadattention_pa_kernel(tc, x, Wq_bytes, Wq_scale, Wk, out_0, out_
 
         def turn(rows, how, in_product_banks=False, wg=None, passes=(0, 1, 2, 3)):
             if wg is None:
-                wg = grouped.tile([P, PASSES, 4 * UNIT], BF16, name="wg", tag="wg", align_bytes=64)
+                wg = grouped.tile([P, PASSES, 4 * UNIT], BF16, name="wg", tag="wg", align_bytes=256)
             waiting = []
             for g in passes:
                 if in_product_banks:
@@ -171,7 +171,7 @@ def tile_multiheadattention_pa_kernel(tc, x, Wq_bytes, Wq_scale, Wk, out_0, out_
                         op=ALU.mult,
                     )
                 elif how[g] == "scalar scaled":
-                    pl = planes.tile([P, 4, UNIT], BF16, name="pl", tag="pl")
+                    pl = planes.tile([P, 4, UNIT], BF16, name="pl", tag="pl", align_bytes=256)
                     tb_v = tb[:].bitcast(BF16).rearrange("p (u n e) -> p u e n", u=2, e=2)
                     for u in range(2):
                         for e in range(2):
@@ -196,8 +196,8 @@ def tile_multiheadattention_pa_kernel(tc, x, Wq_bytes, Wq_scale, Wk, out_0, out_
             return wg
 
         def quantize(wg, pool, tag):
-            wc = pool.tile([P, PASSES, UNIT], U32, name=tag + "c", tag=tag + "c", align_bytes=64)
-            ws = pool.tile([P, PASSES, UNIT], U8, name=tag + "s", tag=tag + "s", align_bytes=64)
+            wc = pool.tile([P, PASSES, UNIT], U32, name=tag + "c", tag=tag + "c", align_bytes=256)
+            ws = pool.tile([P, PASSES, UNIT], U8, name=tag + "s", tag=tag + "s", align_bytes=256)
             nc.vector.quantize_mx(
                 out=wc[:].rearrange("p g n -> p (g n)").bitcast(FP8X4),
                 scales=ws[:].rearrange("p g n -> p (g n)"),
@@ -209,7 +209,7 @@ def tile_multiheadattention_pa_kernel(tc, x, Wq_bytes, Wq_scale, Wk, out_0, out_
 
         def turn_by_matmul(j, scalar_banks, wg, passes):
             if wg is None:
-                wg = grouped.tile([P, PASSES, 4 * UNIT], BF16, name="wg", tag="wg", align_bytes=64)
+                wg = grouped.tile([P, PASSES, 4 * UNIT], BF16, name="wg", tag="wg", align_bytes=256)
             waiting = []
             for g in passes:
                 tb = tpsum.tile([P, 4, UNIT], BF16, name="tb", tag="tb")
@@ -223,7 +223,7 @@ def tile_multiheadattention_pa_kernel(tc, x, Wq_bytes, Wq_scale, Wk, out_0, out_
                             stop=True,
                         )
                 if g < scalar_banks:
-                    pl = planes.tile([P, 4, UNIT], BF16, name="pl", tag="pl")
+                    pl = planes.tile([P, 4, UNIT], BF16, name="pl", tag="pl", align_bytes=256)
                     for t in range(4):
                         nc.scalar.activation(out=pl[:, t, :], in_=tb[:, t, :], func=ACT.Copy, scale=sc[:, g, t : t + 1])
                     waiting.append((g, pl))
@@ -281,7 +281,7 @@ def tile_multiheadattention_pa_kernel(tc, x, Wq_bytes, Wq_scale, Wk, out_0, out_
             )
 
         def finish(ab, out, h0, halves_on):
-            y = res.tile([P, 2, 4, DH], F32, name="y", tag="y")
+            y = res.tile([P, 2, 4, DH], F32, name="y", tag="y", align_bytes=256)
             ab_v = ab[:].rearrange("p w b (a h f j) -> p w h (b a) f j", a=2, h=2, f=2)
             y_v = y[:].rearrange("p h a (f j) -> p h a f j", f=2)
             out_v = out[0, h0 : h0 + 2, :, :].rearrange("h (p a) c -> p h a c", a=4)
@@ -323,7 +323,7 @@ def tile_multiheadattention_pa_kernel(tc, x, Wq_bytes, Wq_scale, Wk, out_0, out_
                 load_q(j + 4)
             if j + 3 < PERIODS:
                 load_k(j + 3)
-            ab_q = prod.tile([P, 2, 2, 512], F32, name="ab", tag="ab")
+            ab_q = prod.tile([P, 2, 2, 512], F32, name="ab", tag="ab", align_bytes=256)
             multiply_rotate(q_codes, ab_q, 0)
             if more:
                 qg = turn_q(j + 1, SCALAR_BANKS[j + 1], passes=(0, 1))
@@ -333,7 +333,7 @@ def tile_multiheadattention_pa_kernel(tc, x, Wq_bytes, Wq_scale, Wk, out_0, out_
                 turn_q(j + 1, SCALAR_BANKS[j + 1], wg=qg, passes=(2, 3))
             if j + 2 < PERIODS:
                 cast_half(j + 2, 1)
-            ab_k = prod.tile([P, 2, 2, 512], F32, name="ab", tag="ab")
+            ab_k = prod.tile([P, 2, 2, 512], F32, name="ab", tag="ab", align_bytes=256)
             multiply_rotate(k_codes, ab_k, 0)
             if more:
                 kg = turn_k(j + 1, passes=(0, 1))

@@ -280,25 +280,27 @@ def tile_multiheadattention_pa_kernel(tc, x, Wq_bytes, Wq_scale, Wk, out_0, out_
                 op=ALU.mult,
             )
 
-        def finish(ab, out, h0, halves_on):
-            y = res.tile([P, 2, 4, DH], F32, name="y", tag="y", align_bytes=256)
+        def result_views(ab, y, out, h0):
             ab_v = ab[:].rearrange("p w b (a h f j) -> p w h (b a) f j", a=2, h=2, f=2)
             y_v = y[:].rearrange("p h a (f j) -> p h a f j", f=2)
             out_v = out[0, h0 : h0 + 2, :, :].rearrange("h (p a) c -> p h a c", a=4)
-            if halves_on is not None:
-                for ap in range(2):
-                    rows = slice(2 * ap, 2 * ap + 2)
-                    for f in range(2):
-                        halves_on.tensor_tensor(
-                            out=y_v[:, :, rows, f, :], in0=ab_v[:, 0, :, rows, f, :], in1=ab_v[:, 1, :, rows, 1 - f, :], op=ALU.add
-                        )
-                    nc.sync.dma_start(out=out_v[:, :, rows, :], in_=y[:, :, rows, :])
-            else:
-                for f in range(2):
-                    nc.gpsimd.tensor_tensor(
-                        out=y_v[:, :, :, f, :], in0=ab_v[:, 0, :, :, f, :], in1=ab_v[:, 1, :, :, 1 - f, :], op=ALU.add
-                    )
-                nc.sync.dma_start(out=out_v, in_=y[:])
+            return ab_v, y_v, out_v
+
+        def finish(ab, out, h0):
+            y = res.tile([P, 2, 4, DH], F32, name="y", tag="y", align_bytes=256)
+            ab_v, y_v, out_v = result_views(ab, y, out, h0)
+            for f in range(2):
+                nc.gpsimd.tensor_tensor(out=y_v[:, :, :, f, :], in0=ab_v[:, 0, :, :, f, :], in1=ab_v[:, 1, :, :, 1 - f, :], op=ALU.add)
+            nc.sync.dma_start(out=out_v, in_=y[:])
+
+        def finish_half(ab, y, out, h0, ap, engine):
+            ab_v, y_v, out_v = result_views(ab, y, out, h0)
+            rows = slice(2 * ap, 2 * ap + 2)
+            for f in range(2):
+                engine.tensor_tensor(
+                    out=y_v[:, :, rows, f, :], in0=ab_v[:, 0, :, rows, f, :], in1=ab_v[:, 1, :, rows, 1 - f, :], op=ALU.add
+                )
+            nc.sync.dma_start(out=out_v[:, :, rows, :], in_=y[:, :, rows, :])
 
         cast_first_unit()
         reduce_angles()
@@ -306,9 +308,9 @@ def tile_multiheadattention_pa_kernel(tc, x, Wq_bytes, Wq_scale, Wk, out_0, out_
         qg = turn_q(0, 0, passes=(2, 3))
         turn_x(0, wg=xg0, passes=(2, 3))
         turn_q(0, 0, wg=qg, passes=(0, 1))
+        x_codes.append(quantize(xg0, xq, "x"))
         q_codes = quantize(qg, codes, "w")
         build_tables()
-        x_codes.append(quantize(xg0, xq, "x"))
         xg1 = turn_x(1)
         x_codes.append(quantize(xg1, xq, "x"))
         kg = turn_k(0)
@@ -317,31 +319,40 @@ def tile_multiheadattention_pa_kernel(tc, x, Wq_bytes, Wq_scale, Wk, out_0, out_
         cast_half(1, 1)
         cast_half(2, 0)
 
-        for j in range(PERIODS):
-            more = j + 1 < PERIODS
+        for j in range(PERIODS - 1):
             if j + 4 < PERIODS:
                 load_q(j + 4)
             if j + 3 < PERIODS:
                 load_k(j + 3)
             ab_q = prod.tile([P, 2, 2, 512], F32, name="ab", tag="ab", align_bytes=256)
             multiply_rotate(q_codes, ab_q, 0)
-            if more:
-                qg = turn_q(j + 1, SCALAR_BANKS[j + 1], passes=(0, 1))
+            qg = turn_q(j + 1, SCALAR_BANKS[j + 1], passes=(0, 1))
             multiply_rotate(q_codes, ab_q, 1)
-            finish(ab_q, out_0, 2 * j, None if more else nc.gpsimd)
-            if more:
-                turn_q(j + 1, SCALAR_BANKS[j + 1], wg=qg, passes=(2, 3))
+            finish(ab_q, out_0, 2 * j)
+            turn_q(j + 1, SCALAR_BANKS[j + 1], wg=qg, passes=(2, 3))
             if j + 2 < PERIODS:
                 cast_half(j + 2, 1)
             ab_k = prod.tile([P, 2, 2, 512], F32, name="ab", tag="ab", align_bytes=256)
             multiply_rotate(k_codes, ab_k, 0)
-            if more:
-                kg = turn_k(j + 1, passes=(0, 1))
-                q_codes = quantize(qg, codes, "w")
+            kg = turn_k(j + 1, passes=(0, 1))
+            q_codes = quantize(qg, codes, "w")
             multiply_rotate(k_codes, ab_k, 1)
-            if more:
-                turn_k(j + 1, wg=kg, passes=(2, 3))
-                k_codes = quantize(kg, codes, "w")
+            turn_k(j + 1, wg=kg, passes=(2, 3))
+            k_codes = quantize(kg, codes, "w")
             if j + 3 < PERIODS:
                 cast_half(j + 3, 0)
-            finish(ab_k, out_1, 2 * j, None if more else nc.vector)
+            finish(ab_k, out_1, 2 * j)
+
+        h_last = 2 * (PERIODS - 1)
+        ab_q = prod.tile([P, 2, 2, 512], F32, name="ab", tag="ab", align_bytes=256)
+        y_q = res.tile([P, 2, 4, DH], F32, name="y", tag="y", align_bytes=256)
+        multiply_rotate(q_codes, ab_q, 0)
+        finish_half(ab_q, y_q, out_0, h_last, 0, nc.gpsimd)
+        multiply_rotate(q_codes, ab_q, 1)
+        ab_k = prod.tile([P, 2, 2, 512], F32, name="ab", tag="ab", align_bytes=256)
+        y_k = res.tile([P, 2, 4, DH], F32, name="y", tag="y", align_bytes=256)
+        multiply_rotate(k_codes, ab_k, 0)
+        finish_half(ab_q, y_q, out_0, h_last, 1, nc.vector)
+        multiply_rotate(k_codes, ab_k, 1)
+        finish_half(ab_k, y_k, out_1, h_last, 0, nc.vector)
+        finish_half(ab_k, y_k, out_1, h_last, 1, nc.vector)

from contextlib import ExitStack
import math

import concourse.mybir as mybir
from concourse.masks import make_identity

S, D, H, DH = 512, 2048, 16, 128
FLOPS = 2 * S * D * (2 * H * DH)

F32 = mybir.dt.float32
BF16 = mybir.dt.bfloat16
I32 = mybir.dt.int32
U32 = mybir.dt.uint32
U8 = mybir.dt.uint8
FP8 = mybir.dt.float8_e4m3fn
FP8X4 = mybir.dt.float8_e4m3fn_x4
ALU = mybir.AluOpType
ACT = mybir.ActivationFunctionType
ENG = mybir.EngineType

P = 128
PASSES = D // 512
UNIT = 256
PERIODS = (H * DH) // UNIT
TURNED_BY_MATMUL = range(1, 7)
TWO_PI = 2.0 * math.pi
SCALAR_BANKS = (0, 1, 2, 2, 2, 2, 2, 2)


def tile_multiheadattention_pa_kernel(tc, x, Wq_bytes, Wq_scale, Wk, out_0, out_1):
    nc = tc.nc
    with ExitStack() as ctx:
        const = ctx.enter_context(tc.tile_pool(name="const", bufs=1))
        xin = ctx.enter_context(tc.tile_pool(name="xin", bufs=8))
        xq = ctx.enter_context(tc.tile_pool(name="xq", bufs=2))
        qbytes = ctx.enter_context(tc.tile_pool(name="qbytes", bufs=4))
        qwide = ctx.enter_context(tc.tile_pool(name="qwide", bufs=3))
        kin = ctx.enter_context(tc.tile_pool(name="kin", bufs=3))
        planes = ctx.enter_context(tc.tile_pool(name="planes", bufs=3))
        grouped = ctx.enter_context(tc.tile_pool(name="grouped", bufs=4))
        codes = ctx.enter_context(tc.tile_pool(name="codes", bufs=4))
        prod = ctx.enter_context(tc.tile_pool(name="prod", bufs=3))
        res = ctx.enter_context(tc.tile_pool(name="res", bufs=3))
        tpsum = ctx.enter_context(tc.psum_pool(name="tpsum", bufs=4))
        mpsum = ctx.enter_context(tc.psum_pool(name="mpsum", bufs=4))
        ctx.enter_context(tc.manual_schedule(engines={ENG.PE, ENG.DVE, ENG.Activation, ENG.Pool}))

        x_rows = x.rearrange("o (p a) k -> p (o a) k", a=4)
        q_rows = Wq_bytes.rearrange("(r p) k -> p r k", p=P)
        k_rows = Wk.rearrange("(r p) k -> p r k", p=P)

        zero = const.tile([P, 1], F32, name="zero", tag="zero")
        warm = const.tile([P, 1], F32, name="warm", tag="warm")
        nc.vector.memset(zero[:], 0.0)
        nc.scalar.activation(out=warm[:], in_=zero[:], func=ACT.Sin)

        ang = const.tile([P, 4, 64], F32, name="ang", tag="ang")
        ang_flat = ang[:].rearrange("p a j -> p (a j)")
        nc.gpsimd.iota(ang_flat, pattern=[[1, 4], [0, 64]], base=0, channel_multiplier=4, allow_small_or_imprecise_dtypes=True)

        ident = const.tile([P, P], F32, name="ident", tag="ident", align_bytes=256)
        make_identity(nc, ident[:])
        ident_b = const.tile([P, P], BF16, name="ident_b", tag="ident_b", align_bytes=256)
        make_identity(nc, ident_b[:])

        q_loaded = {}
        k_loaded = {}

        def load_q(j):
            qb = qbytes.tile([P, 2, D], U8, name="qb", tag="qb", align_bytes=256)
            nc.sync.dma_start(out=qb[:], in_=q_rows[:, 2 * j : 2 * j + 2, :])
            q_loaded[j] = qb

        def load_k(j):
            kb = kin.tile([P, 2, D], BF16, name="kb", tag="kb", align_bytes=256)
            nc.sync.dma_start(out=kb[:], in_=k_rows[:, 2 * j : 2 * j + 2, :])
            k_loaded[j] = kb

        load_q(0)
        x_sb = {}
        sc = const.tile([P, PASSES, 4], F32, name="sc", tag="sc")
        for ap in range(2):
            for g in range(PASSES):
                xt = xin.tile([P, 2, 512], BF16, name="xt", tag="xt", align_bytes=256)
                nc.sync.dma_start(out=xt[:], in_=x_rows[:, 2 * ap : 2 * ap + 2, 512 * g : 512 * (g + 1)])
                x_sb[(ap, g)] = xt
                if ap == 0 and g == 1:
                    nc.sync.dma_start(out=sc[:], in_=Wq_scale.rearrange("o (g p t) -> p (o g) t", p=P, t=4))
        load_k(0)
        load_q(1)
        load_k(1)
        load_q(2)
        load_k(2)
        load_q(3)

        for b in range(6):
            step = 1 << b
            view = ang_flat.rearrange("p (hi two lo) -> p hi two lo", two=2, lo=step)[:, :, 1, :]
            nc.vector.tensor_scalar(out=view, in0=view, scalar1=10000.0 ** (-step / 64.0), scalar2=None, op0=ALU.mult)
        turns_i = const.tile([P, 256], I32, name="turns_i", tag="turns_i")
        red = const.tile([P, 2, 256], F32, name="red", tag="red")
        down = const.tile([P, 256], F32, name="down", tag="down")
        red_s = red[:, 1, :]

        def reduce_angles():
            nc.vector.tensor_scalar(out=turns_i[:], in0=ang_flat, scalar1=1.0 / TWO_PI, scalar2=None, op0=ALU.mult)
            nc.vector.scalar_tensor_tensor(out=red_s, in0=turns_i[:], scalar=-TWO_PI, in1=ang_flat, op0=ALU.mult, op1=ALU.add)
            nc.vector.tensor_scalar(out=down[:], in0=red_s, scalar1=-1.0, scalar2=math.pi / 2.0, op0=ALU.mult, op1=ALU.add)
            nc.vector.scalar_tensor_tensor(out=red[:, 0, :], in0=red_s, scalar=math.pi / 2.0, in1=down[:], op0=ALU.add, op1=ALU.min)

        tab = const.tile([P, 2, 2, 512], F32, name="tab", tag="tab", align_bytes=256)

        trig = const.tile([P, 2, 4, 64], F32, name="trig", tag="trig")

        def build_tables():
            nc.scalar.activation(out=trig[:].rearrange("p w a j -> p (w a j)"), in_=red[:].rearrange("p w c -> p (w c)"), func=ACT.Sin)
            for ap in range(2):
                nc.gpsimd.tensor_scalar(
                    out=tab[:, ap, 0, :].rearrange("p (a m j) -> p a m j", a=2, m=4),
                    in0=trig[:, 0, 2 * ap : 2 * ap + 2, :].unsqueeze(2).to_broadcast([P, 2, 4, 64]),
                    scalar1=1.0,
                    scalar2=0.0,
                    op0=ALU.mult,
                    op1=ALU.add,
                )
                sin_v = tab[:, ap, 1, :].rearrange("p (a h f j) -> p a h f j", a=2, h=2, f=2)
                for f in range(2):
                    nc.gpsimd.tensor_scalar(
                        out=sin_v[:, :, :, f, :],
                        in0=trig[:, 1, 2 * ap : 2 * ap + 2, :].unsqueeze(2).to_broadcast([P, 2, 2, 64]),
                        scalar1=1.0 - 2.0 * f,
                        scalar2=0.0,
                        op0=ALU.mult,
                        op1=ALU.add,
                    )

        q_wide = {}

        def cast_half(j, r):
            if r == 0:
                qf = qwide.tile([P, 2, D], BF16, name="qf", tag="qf", align_bytes=256)
                q_wide[j] = qf
            nc.scalar.copy(out=q_wide[j][:, r, :], in_=q_loaded[j][:, r, :].bitcast(FP8))

        def cast_first_unit():
            qf = qwide.tile([P, 2, D], BF16, name="qf", tag="qf", align_bytes=256)
            q_wide[0] = qf
            for r in range(2):
                nc.scalar.copy(out=qf[:, r, 0 : D // 2], in_=q_loaded[0][:, r, 0 : D // 2].bitcast(FP8))
            for r in range(2):
                nc.vector.tensor_copy(out=qf[:, r, D // 2 : D], in_=q_loaded[0][:, r, D // 2 : D].bitcast(FP8))

        def turn(rows, how, in_product_banks=False, wg=None, passes=(0, 1, 2, 3)):
            if wg is None:
                wg = grouped.tile([P, PASSES, 4 * UNIT], BF16, name="wg", tag="wg", align_bytes=256)
            waiting = []
            for g in passes:
                if in_product_banks:
                    tb = mpsum.tile([P, 2 * UNIT], F32, name="acc", tag="acc")
                else:
                    tb = tpsum.tile([P, 2 * UNIT], F32, name="tb", tag="tb")
                for u in range(2):
                    for r in range(2):
                        c0 = (2 * u + r) * P
                        nc.tensor.transpose(tb[:, c0 : c0 + P], rows(r, g)[:, u:256:2], ident[:])
                if how[g] == "vector scaled":
                    nc.vector.tensor_tensor(
                        out=wg[:, g, :].rearrange("p (n u e) -> p n u e", u=2, e=2),
                        in0=tb[:].bitcast(BF16).rearrange("p (u n e) -> p n u e", u=2, e=2),
                        in1=sc[:, g, :].rearrange("p (u e) -> p u e", u=2).unsqueeze(1).to_broadcast([P, UNIT, 2, 2]),
                        op=ALU.mult,
                    )
                elif how[g] == "scalar scaled":
                    pl = planes.tile([P, 4, UNIT], BF16, name="pl", tag="pl", align_bytes=256)
                    tb_v = tb[:].bitcast(BF16).rearrange("p (u n e) -> p u e n", u=2, e=2)
                    for u in range(2):
                        for e in range(2):
                            t = 2 * u + e
                            nc.scalar.activation(out=pl[:, t, :], in_=tb_v[:, u, e, :], func=ACT.Copy, scale=sc[:, g, t : t + 1])
                    waiting.append((g, pl))
                    if g + 1 == PASSES or how[g + 1] != "scalar scaled":
                        for g_w, pl_w in waiting:
                            nc.scalar.copy(
                                out=wg[:, g_w, :].rearrange("p (n t) -> p n t", t=4), in_=pl_w[:].rearrange("p t n -> p n t")
                            )
                elif how[g] == "vector":
                    nc.vector.tensor_copy(
                        out=wg[:, g, :].bitcast(F32).rearrange("p (n u) -> p n u", u=2),
                        in_=tb[:].rearrange("p (u n) -> p n u", u=2),
                    )
                else:
                    nc.scalar.copy(
                        out=wg[:, g, :].bitcast(F32).rearrange("p (n u) -> p n u", u=2),
                        in_=tb[:].rearrange("p (u n) -> p n u", u=2),
                    )
            return wg

        def quantize(wg, pool, tag):
            wc = pool.tile([P, PASSES, UNIT], U32, name=tag + "c", tag=tag + "c", align_bytes=256)
            ws = pool.tile([P, PASSES, UNIT], U8, name=tag + "s", tag=tag + "s", align_bytes=256)
            nc.vector.quantize_mx(
                out=wc[:].rearrange("p g n -> p (g n)").bitcast(FP8X4),
                scales=ws[:].rearrange("p g n -> p (g n)"),
                in_=wg[:].rearrange("p g c -> p (g c)"),
            )
            return wc, ws

        x_codes = []

        def turn_by_matmul(j, scalar_banks, wg, passes):
            if wg is None:
                wg = grouped.tile([P, PASSES, 4 * UNIT], BF16, name="wg", tag="wg", align_bytes=256)
            waiting = []
            for g in passes:
                tb = tpsum.tile([P, 4, UNIT], BF16, name="tb", tag="tb")
                for r in range(2):
                    for t in range(4):
                        nc.tensor.matmul(
                            out=tb[:, t, r * P : (r + 1) * P],
                            lhsT=q_wide[j][:, r, 512 * g + t : 512 * (g + 1) : 4],
                            rhs=ident_b[:],
                            start=True,
                            stop=True,
                        )
                if g < scalar_banks:
                    pl = planes.tile([P, 4, UNIT], BF16, name="pl", tag="pl", align_bytes=256)
                    for t in range(4):
                        nc.scalar.activation(out=pl[:, t, :], in_=tb[:, t, :], func=ACT.Copy, scale=sc[:, g, t : t + 1])
                    waiting.append((g, pl))
                    if g == passes[-1] or g + 1 == scalar_banks:
                        for g_w, pl_w in waiting:
                            nc.scalar.copy(
                                out=wg[:, g_w, :].rearrange("p (n t) -> p n t", t=4), in_=pl_w[:].rearrange("p t n -> p n t")
                            )
                        waiting = []
                else:
                    nc.vector.tensor_tensor(
                        out=wg[:, g, :].rearrange("p (n t) -> p n t", t=4),
                        in0=tb[:].rearrange("p t n -> p n t"),
                        in1=sc[:, g, :].unsqueeze(1).to_broadcast([P, UNIT, 4]),
                        op=ALU.mult,
                    )
            return wg

        def turn_q(j, scalar_banks, wg=None, passes=(0, 1, 2, 3)):
            if j in TURNED_BY_MATMUL:
                return turn_by_matmul(j, scalar_banks, wg, passes)
            src = q_wide[j]
            how = ["scalar scaled"] * scalar_banks + ["vector scaled"] * (PASSES - scalar_banks)
            return turn(lambda r, g: src[:, r, 512 * g : 512 * (g + 1)].bitcast(F32), how, wg=wg, passes=passes)

        def turn_k(j, wg=None, passes=(0, 1, 2, 3)):
            src = k_loaded[j]
            return turn(lambda r, g: src[:, r, 512 * g : 512 * (g + 1)].bitcast(F32), ["scalar"] * PASSES, wg=wg, passes=passes)

        def turn_x(ap, wg=None, passes=(0, 1, 2, 3)):
            return turn(
                lambda r, g: x_sb[(ap, g)][:, r, :].bitcast(F32), ["scalar"] * PASSES, in_product_banks=True, wg=wg, passes=passes
            )

        def multiply_rotate(w_codes, ab, ap):
            wc, ws = w_codes
            xc, xs = x_codes[ap]
            acc = mpsum.tile([P, 2 * UNIT], F32, name="acc", tag="acc")
            for a2 in range(2):
                for g in range(PASSES):
                    nc.tensor.matmul_mx(
                        out=acc[:, a2 * UNIT : (a2 + 1) * UNIT],
                        lhsT=xc[:, g, a2 * P : (a2 + 1) * P].bitcast(FP8X4),
                        lhsT_scale=xs[:, g, a2 * P : (a2 + 1) * P],
                        rhs=wc[:, g, :].bitcast(FP8X4),
                        rhs_scale=ws[:, g, :],
                        start=(g == 0),
                        stop=(g == PASSES - 1),
                    )
            nc.vector.tensor_tensor(
                out=ab[:, :, ap, :],
                in0=acc[:].unsqueeze(1).to_broadcast([P, 2, 512]),
                in1=tab[:, ap, :, :],
                op=ALU.mult,
            )

        def result_views(ab, y, out, h0):
            ab_v = ab[:].rearrange("p w b (a h f j) -> p w h (b a) f j", a=2, h=2, f=2)
            y_v = y[:].rearrange("p h a (f j) -> p h a f j", f=2)
            out_v = out[0, h0 : h0 + 2, :, :].rearrange("h (p a) c -> p h a c", a=4)
            return ab_v, y_v, out_v

        def finish(ab, out, h0):
            y = res.tile([P, 2, 4, DH], F32, name="y", tag="y", align_bytes=256)
            ab_v, y_v, out_v = result_views(ab, y, out, h0)
            for f in range(2):
                nc.gpsimd.tensor_tensor(out=y_v[:, :, :, f, :], in0=ab_v[:, 0, :, :, f, :], in1=ab_v[:, 1, :, :, 1 - f, :], op=ALU.add)
            nc.sync.dma_start(out=out_v, in_=y[:])

        def finish_half(ab, y, out, h0, ap, engine):
            ab_v, y_v, out_v = result_views(ab, y, out, h0)
            rows = slice(2 * ap, 2 * ap + 2)
            for f in range(2):
                engine.tensor_tensor(
                    out=y_v[:, :, rows, f, :], in0=ab_v[:, 0, :, rows, f, :], in1=ab_v[:, 1, :, rows, 1 - f, :], op=ALU.add
                )
            nc.sync.dma_start(out=out_v[:, :, rows, :], in_=y[:, :, rows, :])

        cast_first_unit()
        reduce_angles()
        xg0 = turn_x(0, passes=(0, 1))
        qg = turn_q(0, 0, passes=(2, 3))
        turn_x(0, wg=xg0, passes=(2, 3))
        turn_q(0, 0, wg=qg, passes=(0, 1))
        x_codes.append(quantize(xg0, xq, "x"))
        q_codes = quantize(qg, codes, "w")
        build_tables()
        xg1 = turn_x(1)
        x_codes.append(quantize(xg1, xq, "x"))
        kg = turn_k(0)
        k_codes = quantize(kg, codes, "w")
        cast_half(1, 0)
        cast_half(1, 1)
        cast_half(2, 0)

        for j in range(PERIODS - 1):
            if j + 4 < PERIODS:
                load_q(j + 4)
            if j + 3 < PERIODS:
                load_k(j + 3)
            ab_q = prod.tile([P, 2, 2, 512], F32, name="ab", tag="ab", align_bytes=256)
            multiply_rotate(q_codes, ab_q, 0)
            qg = turn_q(j + 1, SCALAR_BANKS[j + 1], passes=(0, 1))
            multiply_rotate(q_codes, ab_q, 1)
            finish(ab_q, out_0, 2 * j)
            turn_q(j + 1, SCALAR_BANKS[j + 1], wg=qg, passes=(2, 3))
            if j + 2 < PERIODS:
                cast_half(j + 2, 1)
            ab_k = prod.tile([P, 2, 2, 512], F32, name="ab", tag="ab", align_bytes=256)
            multiply_rotate(k_codes, ab_k, 0)
            kg = turn_k(j + 1, passes=(0, 1))
            q_codes = quantize(qg, codes, "w")
            multiply_rotate(k_codes, ab_k, 1)
            turn_k(j + 1, wg=kg, passes=(2, 3))
            k_codes = quantize(kg, codes, "w")
            if j + 3 < PERIODS:
                cast_half(j + 3, 0)
            finish(ab_k, out_1, 2 * j)

        h_last = 2 * (PERIODS - 1)
        ab_q = prod.tile([P, 2, 2, 512], F32, name="ab", tag="ab", align_bytes=256)
        y_q = res.tile([P, 2, 4, DH], F32, name="y", tag="y", align_bytes=256)
        multiply_rotate(q_codes, ab_q, 0)
        finish_half(ab_q, y_q, out_0, h_last, 0, nc.gpsimd)
        multiply_rotate(q_codes, ab_q, 1)
        ab_k = prod.tile([P, 2, 2, 512], F32, name="ab", tag="ab", align_bytes=256)
        y_k = res.tile([P, 2, 4, DH], F32, name="y", tag="y", align_bytes=256)
        multiply_rotate(k_codes, ab_k, 0)
        finish_half(ab_q, y_q, out_0, h_last, 1, nc.vector)
        multiply_rotate(k_codes, ab_k, 1)
        finish_half(ab_k, y_k, out_1, h_last, 0, nc.vector)
        finish_half(ab_k, y_k, out_1, h_last, 1, nc.vector)
